import numpy as np
import ml_dtypes


def mxq(x, axis, fmt="e4m3"):
    dtype, down = {"e4m3": (ml_dtypes.float8_e4m3fn, 7), "e5m2": (ml_dtypes.float8_e5m2, 14)}[fmt]
    v = np.moveaxis(np.asarray(x, np.float32).astype(ml_dtypes.bfloat16).astype(np.float64), axis, -1)
    blocks = v.reshape(v.shape[:-1] + (-1, 32))
    amax = np.abs(blocks).max(-1, keepdims=True)
    byte = np.maximum(np.where(amax > 0, np.frexp(amax)[1] - 1 + 127, 0) - down, 1)
    scale = np.exp2(byte - 127.0)
    codes = (blocks / scale).astype(np.float32).astype(dtype).astype(np.float64)
    return np.moveaxis((codes * scale).reshape(v.shape), -1, axis)


WIDE = False


def mx_kscale(k):
    if not WIDE:
        return np.ones(k)
    levels = np.array([20, -20, 10, -10, 0])
    a = np.random.permutation(np.resize(levels, k // 512 * 4)).reshape(k // 512, 4)
    idx = np.arange(k)
    return np.exp2(a[idx // 512, idx % 128 // 32])


BF16 = ml_dtypes.bfloat16


def bf(x):
    return np.asarray(x, np.float32).astype(BF16)


def f64(x):
    return np.asarray(x).astype(np.float64)


B, S, D_IN, D_OUT = 3, 512, 256, 8192


def relative_shift(x):
    b, s, d = x.shape
    padded = np.concatenate([np.zeros((b, 1, d)), x], axis=1).reshape(s + 1, b, d)
    return padded[1:].reshape(b, s, d)


def relative_shift_adjoint(g, b, s):
    d = g.shape[1]
    padded = np.concatenate([np.zeros((b, d)), g], axis=0).reshape(b, s + 1, d)
    return padded[:, 1:]


def setup_inputs():
    u = mx_kscale(D_OUT)
    pos_embed = np.random.standard_normal((B, S, D_IN))
    W_r = np.random.standard_normal((D_OUT, D_IN)) * 1.2 / np.sqrt(D_IN) / u[:, None]
    b_r = np.random.standard_normal(D_OUT) * 0.3
    g = np.random.standard_normal((B, S, D_OUT)) * np.exp2(np.random.randint(-12, 1, (B, S, 1))) * 8.0 * u
    return {"pos_embed": bf(pos_embed), "W_r": bf(W_r), "b_r": bf(b_r), "grad_out": bf(g)}


def reference(pos_embed, W_r, b_r, grad_out):
    g = f64(grad_out).reshape(B * S, D_OUT)
    gs = mxq(g, 1, "e5m2") @ mxq(f64(W_r), 0, "e4m3")
    return relative_shift_adjoint(gs, B, S)

@@ -1,0 +1,217 @@
+from contextlib import ExitStack
+
+import concourse.mybir as mybir
+from concourse.masks import make_identity
+
+F32 = mybir.dt.float32
+BF16 = mybir.dt.bfloat16
+U32 = mybir.dt.uint32
+U8 = mybir.dt.uint8
+E4M3X4 = mybir.dt.float8_e4m3fn_x4
+E5M2X4 = mybir.dt.float8_e5m2_x4
+
+BATCH, SEQ, D_IN, D_OUT = 3, 512, 256, 8192
+TOKENS = BATCH * SEQ
+
+P = 128
+PACK = 4
+K_PASS = P * PACK
+PASSES = D_OUT // K_PASS
+GROUP = 512
+GROUPS = TOKENS // GROUP
+SUBTILES = GROUP // P
+M_TILES = D_IN // P
+HALF_WORDS = K_PASS // 4
+
+LOAD_PASSES = 4
+LOAD_K = LOAD_PASSES * K_PASS
+LOADS = PASSES // LOAD_PASSES
+RUN_PASSES = 2
+GRAD_BUFS = 6
+
+FLOPS = 2 * TOKENS * D_OUT * D_IN
+BYTES = 2 * TOKENS * D_OUT + 2 * D_OUT * D_IN + 4 * TOKENS * D_IN
+
+
+def tile_relativemultiheadattention_pa_k_kernel(tc, pos_embed, W_r, b_r, grad_out, out):
+    nc = tc.nc
+    grad_rows = grad_out.flatten_outer_dims()
+    out_rows = out.flatten_outer_dims()
+
+    with ExitStack() as ctx:
+        keep = ctx.enter_context(tc.tile_pool(name="keep", bufs=1))
+        grad_pool = ctx.enter_context(tc.tile_pool(name="grad", bufs=GRAD_BUFS))
+        w_raw_pool = ctx.enter_context(tc.tile_pool(name="w_raw", bufs=LOADS))
+        w_grouped_pool = ctx.enter_context(tc.tile_pool(name="w_grouped", bufs=2))
+        grouped_pool = ctx.enter_context(tc.tile_pool(name="grouped", bufs=2 * RUN_PASSES))
+        operand_pool = ctx.enter_context(tc.tile_pool(name="operand", bufs=3 * RUN_PASSES))
+        result_pool = ctx.enter_context(tc.tile_pool(name="result", bufs=4))
+        acc_pool = ctx.enter_context(tc.psum_pool(name="acc", bufs=1))
+        bank_pool = ctx.enter_context(tc.psum_pool(name="bank", bufs=8 - M_TILES))
+        ctx.enter_context(tc.manual_schedule())
+
+        identity = keep.tile([P, P], F32, name="identity")
+        make_identity(nc, identity[:])
+
+        w_codes = keep.tile([P, PASSES, D_IN], U32, name="w_codes", align_bytes=64)
+        w_scales = keep.tile([P, PASSES, D_IN], U8, name="w_scales", align_bytes=64)
+
+        g_t = [keep.tile([P, TOKENS], F32, name="g_t%d" % m) for m in range(M_TILES)]
+        for m in range(M_TILES):
+            nc.vector.memset(g_t[m][:, 0:8], 0.0)
+
+        def load_grad(index):
+            n, q = divmod(index, LOADS)
+            raw = grad_pool.tile([P, SUBTILES, LOAD_K], BF16, name="grad_raw")
+            rows = grad_rows[n * GROUP : (n + 1) * GROUP, q * LOAD_K : (q + 1) * LOAD_K]
+            nc.sync.dma_start(out=raw[:], in_=rows.rearrange("(s p) k -> p s k", p=P))
+            return raw
+
+        def load_weights(q):
+            raw = w_raw_pool.tile([P, LOAD_PASSES, PACK, D_IN], BF16, name="w_raw")
+            rows = W_r[q * LOAD_K : (q + 1) * LOAD_K, :]
+            nc.sync.dma_start(
+                out=raw[:].rearrange("p g (u e) d -> p (g u) (e d)", e=2),
+                in_=rows.rearrange("(g u p e) d -> p (g u) (e d)", u=2, p=P, e=2),
+            )
+            return raw
+
+        def regroup_weights(raw, first_pass):
+            grouped = w_grouped_pool.tile([P, RUN_PASSES, D_IN, PACK], BF16, name="w_grouped", align_bytes=64)
+            for j in range(RUN_PASSES):
+                nc.vector.tensor_copy(
+                    out=grouped[:, j, :, :].rearrange("p (c i) t -> p c t i", i=4),
+                    in_=raw[:, first_pass % LOAD_PASSES + j, :, :].rearrange("p t (c i) -> p c t i", i=4),
+                )
+            return grouped
+
+        def quantise_weights(grouped, first_pass):
+            passes = slice(first_pass, first_pass + RUN_PASSES)
+            nc.vector.quantize_mx(
+                out=w_codes[:, passes, :].rearrange("p c d -> p (c d)").bitcast(E4M3X4),
+                scales=w_scales[:, passes, :].rearrange("p c d -> p (c d)"),
+                in_=grouped[:].rearrange("p c d t -> p (c d t)"),
+            )
+
+        def transpose_run(raw, n, first_pass):
+            operands = []
+            grouped_tiles = []
+            for j in range(RUN_PASSES):
+                word0 = ((first_pass + j) % LOAD_PASSES) * 2 * HALF_WORDS
+                grouped = grouped_pool.tile([P, GROUP, PACK], BF16, name="grouped", align_bytes=64)
+                grouped_tiles.append(grouped)
+                for half in range(2):
+                    bank = bank_pool.tile([P, 2, 2 * P], F32, name="bank")
+                    for u in range(2):
+                        for s in range(2):
+                            words = raw[:, 2 * half + s, :].bitcast(F32)
+                            nc.tensor.transpose(
+                                bank[:, u, s * P : (s + 1) * P],
+                                words[:, word0 + u * HALF_WORDS : word0 + (u + 1) * HALF_WORDS],
+                                identity[:],
+                            )
+                    tokens = slice(half * 2 * P, (half + 1) * 2 * P)
+                    pairs = (
+                        grouped[:, tokens, :]
+                        .rearrange("p r t -> p (r t)")
+                        .bitcast(F32)
+                        .rearrange("p (r u) -> p r u", u=2)
+                    )
+                    if n > 0 and j == RUN_PASSES - 1 and half == 1:
+                        nc.vector.tensor_copy(out=pairs, in_=bank[:].rearrange("p u r -> p r u"))
+                    else:
+                        nc.scalar.copy(out=pairs, in_=bank[:].rearrange("p u r -> p r u"))
+            for j in range(RUN_PASSES):
+                codes = operand_pool.tile([P, GROUP], U32, name="grad_codes", align_bytes=64)
+                scales = operand_pool.tile([P, GROUP], U8, name="grad_scales", align_bytes=64)
+                nc.vector.quantize_mx(
+                    out=codes[:].bitcast(E5M2X4),
+                    scales=scales[:],
+                    in_=grouped_tiles[j][:].rearrange("p r t -> p (r t)"),
+                )
+                operands.append((first_pass + j, codes, scales))
+            return operands
+
+        def multiply_run(operands, acc):
+            for c, codes, scales in operands:
+                for m in range(M_TILES):
+                    columns = slice(m * P, (m + 1) * P)
+                    nc.tensor.matmul_mx(
+                        out=acc[m][:],
+                        lhsT=w_codes[:, c, columns].bitcast(E4M3X4),
+                        lhsT_scale=w_scales[:, c, columns],
+                        rhs=codes[:].bitcast(E5M2X4),
+                        rhs_scale=scales[:],
+                        start=(c == 0),
+                        stop=(c == PASSES - 1),
+                    )
+
+        def shift_out_of_psum(n, acc):
+            for m in range(M_TILES):
+                for b in range(BATCH):
+                    first_s = max(0, 2 - (SEQ + 1) * b)
+                    lo = max((SEQ + 1) * b + first_s - 2, n * GROUP)
+                    hi = min((SEQ + 1) * b + SEQ - 2, (n + 1) * GROUP)
+                    if lo < hi:
+                        src = acc[m][:, lo - n * GROUP : hi - n * GROUP]
+                        dst = g_t[m][:, lo + 2 - b : hi + 2 - b]
+                        if m == 0:
+                            nc.scalar.copy(out=dst, in_=src)
+                        else:
+                            nc.vector.tensor_copy(out=dst, in_=src)
+
+        def store_group(n):
+            for pair in range(SUBTILES // 2):
+                row0 = n * GROUP + pair * 2 * P
+                bank = bank_pool.tile([P, 2, D_IN], F32, name="bank")
+                for j in range(2):
+                    for m in range(M_TILES):
+                        nc.tensor.transpose(
+                            bank[:, j, m * P : (m + 1) * P],
+                            g_t[m][:, row0 + j * P : row0 + (j + 1) * P],
+                            identity[:],
+                        )
+                result = result_pool.tile([P, 2, D_IN], F32, name="result")
+                if pair == 0:
+                    nc.scalar.copy(out=result[:], in_=bank[:])
+                else:
+                    nc.vector.tensor_copy(out=result[:], in_=bank[:])
+                nc.sync.dma_start(
+                    out=out_rows[row0 : row0 + 2 * P, :].rearrange("(j p) d -> p j d", p=P),
+                    in_=result[:],
+                )
+
+        grad_tiles = {}
+        w_tiles = {}
+        for index in range(GRAD_BUFS):
+            grad_tiles[index] = load_grad(index)
+            if index < LOADS:
+                w_tiles[index] = load_weights(index)
+
+        acc = None
+        waiting = None
+        to_store = None
+        for n in range(GROUPS):
+            for first_pass in range(0, PASSES, RUN_PASSES):
+                index = n * LOADS + first_pass // LOAD_PASSES
+                if n == 0:
+                    w_grouped = regroup_weights(w_tiles[index], first_pass)
+                operands = transpose_run(grad_tiles[index], n, first_pass)
+                if n == 0:
+                    quantise_weights(w_grouped, first_pass)
+                if (first_pass + RUN_PASSES) % LOAD_PASSES == 0 and index + GRAD_BUFS < GROUPS * LOADS:
+                    grad_tiles[index + GRAD_BUFS] = load_grad(index + GRAD_BUFS)
+                if to_store is not None:
+                    store_group(to_store)
+                    to_store = None
+                if waiting is not None:
+                    multiply_run(waiting, acc)
+                    if first_pass == 0:
+                        shift_out_of_psum(n - 1, acc)
+                        to_store = n - 1
+                if first_pass == 0:
+                    acc = [acc_pool.tile([P, GROUP], F32, name="acc%d" % m) for m in range(M_TILES)]
+                waiting = operands
+        multiply_run(waiting, acc)
+        shift_out_of_psum(GROUPS - 1, acc)
+        store_group(GROUPS - 1)

@@ -26,8 +26,8 @@ HALF_WORDS = K_PASS // 4
 LOAD_PASSES = 4
 LOAD_K = LOAD_PASSES * K_PASS
 LOADS = PASSES // LOAD_PASSES
-RUN_PASSES = 2
-GRAD_BUFS = 6
+RUN_PASSES = 4
+GRAD_BUFS = 5
 
 FLOPS = 2 * TOKENS * D_OUT * D_IN
 BYTES = 2 * TOKENS * D_OUT + 2 * D_OUT * D_IN + 4 * TOKENS * D_IN
@@ -43,8 +43,8 @@ def tile_relativemultiheadattention_pa_k_kernel(tc, pos_embed, W_r, b_r, grad_ou
         grad_pool = ctx.enter_context(tc.tile_pool(name="grad", bufs=GRAD_BUFS))
         w_raw_pool = ctx.enter_context(tc.tile_pool(name="w_raw", bufs=LOADS))
         w_grouped_pool = ctx.enter_context(tc.tile_pool(name="w_grouped", bufs=2))
-        grouped_pool = ctx.enter_context(tc.tile_pool(name="grouped", bufs=2 * RUN_PASSES))
-        operand_pool = ctx.enter_context(tc.tile_pool(name="operand", bufs=3 * RUN_PASSES))
+        grouped_pool = ctx.enter_context(tc.tile_pool(name="grouped", bufs=RUN_PASSES + 2))
+        operand_pool = ctx.enter_context(tc.tile_pool(name="operand", bufs=2 * RUN_PASSES + 1))
         result_pool = ctx.enter_context(tc.tile_pool(name="result", bufs=4))
         acc_pool = ctx.enter_context(tc.psum_pool(name="acc", bufs=1))
         bank_pool = ctx.enter_context(tc.psum_pool(name="bank", bufs=8 - M_TILES))
@@ -96,6 +96,17 @@ def tile_relativemultiheadattention_pa_k_kernel(tc, pos_embed, W_r, b_r, grad_ou
         def transpose_run(raw, n, first_pass):
             operands = []
             grouped_tiles = []
+
+            def quantise_pass(j):
+                codes = operand_pool.tile([P, GROUP], U32, name="grad_codes", align_bytes=64)
+                scales = operand_pool.tile([P, GROUP], U8, name="grad_scales", align_bytes=64)
+                nc.vector.quantize_mx(
+                    out=codes[:].bitcast(E5M2X4),
+                    scales=scales[:],
+                    in_=grouped_tiles[j][:].rearrange("p r t -> p (r t)"),
+                )
+                operands.append((first_pass + j, codes, scales))
+
             for j in range(RUN_PASSES):
                 word0 = ((first_pass + j) % LOAD_PASSES) * 2 * HALF_WORDS
                 grouped = grouped_pool.tile([P, GROUP, PACK], BF16, name="grouped", align_bytes=64)
@@ -117,19 +128,13 @@ def tile_relativemultiheadattention_pa_k_kernel(tc, pos_embed, W_r, b_r, grad_ou
                         .bitcast(F32)
                         .rearrange("p (r u) -> p r u", u=2)
                     )
-                    if n > 0 and j == RUN_PASSES - 1 and half == 1:
+                    if n > 0 and j % 2 == 1 and half == 1:
                         nc.vector.tensor_copy(out=pairs, in_=bank[:].rearrange("p u r -> p r u"))
                     else:
                         nc.scalar.copy(out=pairs, in_=bank[:].rearrange("p u r -> p r u"))
-            for j in range(RUN_PASSES):
-                codes = operand_pool.tile([P, GROUP], U32, name="grad_codes", align_bytes=64)
-                scales = operand_pool.tile([P, GROUP], U8, name="grad_scales", align_bytes=64)
-                nc.vector.quantize_mx(
-                    out=codes[:].bitcast(E5M2X4),
-                    scales=scales[:],
-                    in_=grouped_tiles[j][:].rearrange("p r t -> p (r t)"),
-                )
-                operands.append((first_pass + j, codes, scales))
+                if j > 0:
+                    quantise_pass(j - 1)
+            quantise_pass(RUN_PASSES - 1)
             return operands
 
         def multiply_run(operands, acc):

@@ -19,15 +19,17 @@ K_PASS = P * PACK
 PASSES = D_OUT // K_PASS
 GROUP = 512
 GROUPS = TOKENS // GROUP
-SUBTILES = GROUP // P
+HALF = GROUP // 2
 M_TILES = D_IN // P
-HALF_WORDS = K_PASS // 4
+PLANE = K_PASS // 4
 
-LOAD_PASSES = 4
-LOAD_K = LOAD_PASSES * K_PASS
-LOADS = PASSES // LOAD_PASSES
-RUN_PASSES = 4
-GRAD_BUFS = 5
+CHUNK_PASSES = 4
+CHUNK_K = CHUNK_PASSES * K_PASS
+K_CHUNKS = PASSES // CHUNK_PASSES
+TOGETHER = 2
+PSUM_BANKS = 8
+CHUNKS_AHEAD = 5
+PAD = 8
 
 FLOPS = 2 * TOKENS * D_OUT * D_IN
 BYTES = 2 * TOKENS * D_OUT + 2 * D_OUT * D_IN + 4 * TOKENS * D_IN
@@ -37,17 +39,21 @@ def tile_relativemultiheadattention_pa_k_kernel(tc, pos_embed, W_r, b_r, grad_ou
     nc = tc.nc
     grad_rows = grad_out.flatten_outer_dims()
     out_rows = out.flatten_outer_dims()
+    assert SEQ == GROUP
+
+    chunks = [(n, q) for q in range(K_CHUNKS) for n in range(TOGETHER)]
+    chunks += [(n, q) for n in range(TOGETHER, GROUPS) for q in range(K_CHUNKS)]
 
     with ExitStack() as ctx:
         keep = ctx.enter_context(tc.tile_pool(name="keep", bufs=1))
-        grad_pool = ctx.enter_context(tc.tile_pool(name="grad", bufs=GRAD_BUFS))
-        w_raw_pool = ctx.enter_context(tc.tile_pool(name="w_raw", bufs=LOADS))
+        grad_pool = ctx.enter_context(tc.tile_pool(name="grad", bufs=2 * CHUNKS_AHEAD))
+        w_raw_pool = ctx.enter_context(tc.tile_pool(name="w_raw", bufs=K_CHUNKS))
         w_grouped_pool = ctx.enter_context(tc.tile_pool(name="w_grouped", bufs=2))
-        grouped_pool = ctx.enter_context(tc.tile_pool(name="grouped", bufs=RUN_PASSES + 2))
-        operand_pool = ctx.enter_context(tc.tile_pool(name="operand", bufs=2 * RUN_PASSES + 1))
+        grouped_pool = ctx.enter_context(tc.tile_pool(name="grouped", bufs=CHUNK_PASSES + 2))
+        operand_pool = ctx.enter_context(tc.tile_pool(name="operand", bufs=2 * CHUNK_PASSES + 1))
         result_pool = ctx.enter_context(tc.tile_pool(name="result", bufs=4))
-        acc_pool = ctx.enter_context(tc.psum_pool(name="acc", bufs=1))
-        bank_pool = ctx.enter_context(tc.psum_pool(name="bank", bufs=8 - M_TILES))
+        acc_pool = ctx.enter_context(tc.psum_pool(name="acc", bufs=TOGETHER))
+        bank_pool = ctx.enter_context(tc.psum_pool(name="bank", bufs=PSUM_BANKS - TOGETHER * M_TILES))
         ctx.enter_context(tc.manual_schedule())
 
         identity = keep.tile([P, P], F32, name="identity")
@@ -56,46 +62,58 @@ def tile_relativemultiheadattention_pa_k_kernel(tc, pos_embed, W_r, b_r, grad_ou
         w_codes = keep.tile([P, PASSES, D_IN], U32, name="w_codes", align_bytes=64)
         w_scales = keep.tile([P, PASSES, D_IN], U8, name="w_scales", align_bytes=64)
 
-        g_t = [keep.tile([P, TOKENS], F32, name="g_t%d" % m) for m in range(M_TILES)]
+        g_t = [keep.tile([P, PAD + TOKENS], F32, name="g_t%d" % m) for m in range(M_TILES)]
         for m in range(M_TILES):
-            nc.vector.memset(g_t[m][:, 0:8], 0.0)
+            nc.vector.memset(g_t[m][:, 0:PAD], 0.0)
 
-        def load_grad(index):
-            n, q = divmod(index, LOADS)
-            raw = grad_pool.tile([P, SUBTILES, LOAD_K], BF16, name="grad_raw")
-            rows = grad_rows[n * GROUP : (n + 1) * GROUP, q * LOAD_K : (q + 1) * LOAD_K]
-            nc.sync.dma_start(out=raw[:], in_=rows.rearrange("(s p) k -> p s k", p=P))
-            return raw
+        w_raw = {}
+        grad_raw = {}
+        acc = {}
 
-        def load_weights(q):
-            raw = w_raw_pool.tile([P, LOAD_PASSES, PACK, D_IN], BF16, name="w_raw")
-            rows = W_r[q * LOAD_K : (q + 1) * LOAD_K, :]
-            nc.sync.dma_start(
-                out=raw[:].rearrange("p g (u e) d -> p (g u) (e d)", e=2),
-                in_=rows.rearrange("(g u p e) d -> p (g u) (e d)", u=2, p=P, e=2),
-            )
-            return raw
+        def load_chunk(i):
+            n, q = chunks[i]
+            k_range = slice(q * CHUNK_K, (q + 1) * CHUNK_K)
+            if n == 0:
+                raw = w_raw_pool.tile([P, CHUNK_PASSES, PACK, D_IN], BF16, name="w_raw")
+                nc.sync.dma_start(
+                    out=raw[:].rearrange("p g (u e) d -> p (g u) (e d)", e=2),
+                    in_=W_r[k_range, :].rearrange("(g u p e) d -> p (g u) (e d)", u=2, p=P, e=2),
+                )
+                w_raw[q] = raw
+            grad_raw[i] = []
+            for h in range(GROUP // HALF):
+                raw = grad_pool.tile([P, HALF // P, CHUNK_K], BF16, name="grad_raw")
+                row0 = n * GROUP + h * HALF
+                nc.sync.dma_start(
+                    out=raw[:],
+                    in_=grad_rows[row0 : row0 + HALF, k_range].rearrange("(s p) k -> p s k", p=P),
+                )
+                grad_raw[i].append(raw)
 
-        def regroup_weights(raw, first_pass):
-            grouped = w_grouped_pool.tile([P, RUN_PASSES, D_IN, PACK], BF16, name="w_grouped", align_bytes=64)
-            for j in range(RUN_PASSES):
+        def regroup_weights(q):
+            grouped = w_grouped_pool.tile([P, CHUNK_PASSES, D_IN, PACK], BF16, name="w_grouped", align_bytes=64)
+            for j in range(CHUNK_PASSES):
                 nc.vector.tensor_copy(
                     out=grouped[:, j, :, :].rearrange("p (c i) t -> p c t i", i=4),
-                    in_=raw[:, first_pass % LOAD_PASSES + j, :, :].rearrange("p t (c i) -> p c t i", i=4),
+                    in_=w_raw[q][:, j, :, :].rearrange("p t (c i) -> p c t i", i=4),
                 )
             return grouped
 
-        def quantise_weights(grouped, first_pass):
-            passes = slice(first_pass, first_pass + RUN_PASSES)
+        def quantise_weights(q, grouped):
+            passes = slice(q * CHUNK_PASSES, (q + 1) * CHUNK_PASSES)
             nc.vector.quantize_mx(
                 out=w_codes[:, passes, :].rearrange("p c d -> p (c d)").bitcast(E4M3X4),
                 scales=w_scales[:, passes, :].rearrange("p c d -> p (c d)"),
                 in_=grouped[:].rearrange("p c d t -> p (c d t)"),
             )
 
-        def transpose_run(raw, n, first_pass):
+        def transpose_chunk(i):
+            n, q = chunks[i]
+            grouped = [
+                grouped_pool.tile([P, GROUP, PACK], BF16, name="grouped", align_bytes=64)
+                for j in range(CHUNK_PASSES)
+            ]
             operands = []
-            grouped_tiles = []
 
             def quantise_pass(j):
                 codes = operand_pool.tile([P, GROUP], U32, name="grad_codes", align_bytes=64)
@@ -103,46 +121,45 @@ def tile_relativemultiheadattention_pa_k_kernel(tc, pos_embed, W_r, b_r, grad_ou
                 nc.vector.quantize_mx(
                     out=codes[:].bitcast(E5M2X4),
                     scales=scales[:],
-                    in_=grouped_tiles[j][:].rearrange("p r t -> p (r t)"),
+                    in_=grouped[j][:].rearrange("p r t -> p (r t)"),
                 )
-                operands.append((first_pass + j, codes, scales))
+                operands.append((q * CHUNK_PASSES + j, codes, scales))
 
-            for j in range(RUN_PASSES):
-                word0 = ((first_pass + j) % LOAD_PASSES) * 2 * HALF_WORDS
-                grouped = grouped_pool.tile([P, GROUP, PACK], BF16, name="grouped", align_bytes=64)
-                grouped_tiles.append(grouped)
-                for half in range(2):
-                    bank = bank_pool.tile([P, 2, 2 * P], F32, name="bank")
+            for h in range(GROUP // HALF):
+                for j in range(CHUNK_PASSES):
+                    bank = bank_pool.tile([P, 2, HALF], F32, name="bank")
                     for u in range(2):
-                        for s in range(2):
-                            words = raw[:, 2 * half + s, :].bitcast(F32)
+                        for s in range(HALF // P):
+                            word0 = (2 * j + u) * PLANE
                             nc.tensor.transpose(
                                 bank[:, u, s * P : (s + 1) * P],
-                                words[:, word0 + u * HALF_WORDS : word0 + (u + 1) * HALF_WORDS],
+                                grad_raw[i][h][:, s, :].bitcast(F32)[:, word0 : word0 + PLANE],
                                 identity[:],
                             )
-                    tokens = slice(half * 2 * P, (half + 1) * 2 * P)
                     pairs = (
-                        grouped[:, tokens, :]
+                        grouped[j][:, h * HALF : (h + 1) * HALF, :]
                         .rearrange("p r t -> p (r t)")
                         .bitcast(F32)
                         .rearrange("p (r u) -> p r u", u=2)
                     )
-                    if n > 0 and j % 2 == 1 and half == 1:
+                    if n >= TOGETHER and j == CHUNK_PASSES - 1:
                         nc.vector.tensor_copy(out=pairs, in_=bank[:].rearrange("p u r -> p r u"))
                     else:
                         nc.scalar.copy(out=pairs, in_=bank[:].rearrange("p u r -> p r u"))
-                if j > 0:
-                    quantise_pass(j - 1)
-            quantise_pass(RUN_PASSES - 1)
+                    if h == 1 and j > 0:
+                        quantise_pass(j - 1)
+            quantise_pass(CHUNK_PASSES - 1)
             return operands
 
-        def multiply_run(operands, acc):
-            for c, codes, scales in operands:
-                for m in range(M_TILES):
-                    columns = slice(m * P, (m + 1) * P)
+        def multiply_chunk(i, operands):
+            n, q = chunks[i]
+            if q == 0:
+                acc[n] = [acc_pool.tile([P, GROUP], F32, name="acc%d" % m) for m in range(M_TILES)]
+            for m in range(M_TILES):
+                columns = slice(m * P, (m + 1) * P)
+                for c, codes, scales in operands:
                     nc.tensor.matmul_mx(
-                        out=acc[m][:],
+                        out=acc[n][m][:],
                         lhsT=w_codes[:, c, columns].bitcast(E4M3X4),
                         lhsT_scale=w_scales[:, c, columns],
                         rhs=codes[:].bitcast(E5M2X4),
@@ -150,73 +167,58 @@ def tile_relativemultiheadattention_pa_k_kernel(tc, pos_embed, W_r, b_r, grad_ou
                         start=(c == 0),
                         stop=(c == PASSES - 1),
                     )
+                if q == K_CHUNKS - 1:
+                    done = g_t[m][:, PAD + n * GROUP : PAD + (n + 1) * GROUP]
+                    if m == 0:
+                        nc.scalar.copy(out=done, in_=acc[n][m][:])
+                    else:
+                        nc.vector.tensor_copy(out=done, in_=acc[n][m][:])
 
-        def shift_out_of_psum(n, acc):
+        def store_batch(b):
+            banks = [bank_pool.tile([P, 2, D_IN], F32, name="bank") for pair in range(2)]
             for m in range(M_TILES):
-                for b in range(BATCH):
-                    first_s = max(0, 2 - (SEQ + 1) * b)
-                    lo = max((SEQ + 1) * b + first_s - 2, n * GROUP)
-                    hi = min((SEQ + 1) * b + SEQ - 2, (n + 1) * GROUP)
-                    if lo < hi:
-                        src = acc[m][:, lo - n * GROUP : hi - n * GROUP]
-                        dst = g_t[m][:, lo + 2 - b : hi + 2 - b]
-                        if m == 0:
-                            nc.scalar.copy(out=dst, in_=src)
-                        else:
-                            nc.vector.tensor_copy(out=dst, in_=src)
-
-        def store_group(n):
-            for pair in range(SUBTILES // 2):
-                row0 = n * GROUP + pair * 2 * P
-                bank = bank_pool.tile([P, 2, D_IN], F32, name="bank")
-                for j in range(2):
-                    for m in range(M_TILES):
+                for pair in range(2):
+                    for j in range(2):
+                        s0 = (2 * pair + j) * P
+                        col0 = PAD + (SEQ + 1) * b + s0 - 2
                         nc.tensor.transpose(
-                            bank[:, j, m * P : (m + 1) * P],
-                            g_t[m][:, row0 + j * P : row0 + (j + 1) * P],
+                            banks[pair][:, j, m * P : (m + 1) * P],
+                            g_t[m][:, col0 : col0 + P],
                             identity[:],
                         )
+            for pair in range(2):
                 result = result_pool.tile([P, 2, D_IN], F32, name="result")
                 if pair == 0:
-                    nc.scalar.copy(out=result[:], in_=bank[:])
+                    nc.scalar.copy(out=result[:], in_=banks[pair][:])
                 else:
-                    nc.vector.tensor_copy(out=result[:], in_=bank[:])
+                    nc.vector.tensor_copy(out=result[:], in_=banks[pair][:])
+                row0 = b * SEQ + pair * 2 * P
                 nc.sync.dma_start(
                     out=out_rows[row0 : row0 + 2 * P, :].rearrange("(j p) d -> p j d", p=P),
                     in_=result[:],
                 )
 
-        grad_tiles = {}
-        w_tiles = {}
-        for index in range(GRAD_BUFS):
-            grad_tiles[index] = load_grad(index)
-            if index < LOADS:
-                w_tiles[index] = load_weights(index)
+        for i in range(CHUNKS_AHEAD):
+            load_chunk(i)
 
-        acc = None
         waiting = None
-        to_store = None
-        for n in range(GROUPS):
-            for first_pass in range(0, PASSES, RUN_PASSES):
-                index = n * LOADS + first_pass // LOAD_PASSES
-                if n == 0:
-                    w_grouped = regroup_weights(w_tiles[index], first_pass)
-                operands = transpose_run(grad_tiles[index], n, first_pass)
-                if n == 0:
-                    quantise_weights(w_grouped, first_pass)
-                if (first_pass + RUN_PASSES) % LOAD_PASSES == 0 and index + GRAD_BUFS < GROUPS * LOADS:
-                    grad_tiles[index + GRAD_BUFS] = load_grad(index + GRAD_BUFS)
-                if to_store is not None:
-                    store_group(to_store)
-                    to_store = None
-                if waiting is not None:
-                    multiply_run(waiting, acc)
-                    if first_pass == 0:
-                        shift_out_of_psum(n - 1, acc)
-                        to_store = n - 1
-                if first_pass == 0:
-                    acc = [acc_pool.tile([P, GROUP], F32, name="acc%d" % m) for m in range(M_TILES)]
-                waiting = operands
-        multiply_run(waiting, acc)
-        shift_out_of_psum(GROUPS - 1, acc)
-        store_group(GROUPS - 1)
+        complete = []
+        for i in range(len(chunks)):
+            n, q = chunks[i]
+            if n == 0:
+                w_grouped = regroup_weights(q)
+            operands = transpose_chunk(i)
+            if n == 0:
+                quantise_weights(q, w_grouped)
+            if i + CHUNKS_AHEAD < len(chunks):
+                load_chunk(i + CHUNKS_AHEAD)
+            for b in complete:
+                store_batch(b)
+            complete = []
+            if i > 0:
+                multiply_chunk(i - 1, waiting)
+                if chunks[i - 1][1] == K_CHUNKS - 1:
+                    complete.append(chunks[i - 1][0])
+            waiting = operands
+        multiply_chunk(len(chunks) - 1, waiting)
+        store_batch(GROUPS - 1)

from contextlib import ExitStack

import concourse.mybir as mybir
from concourse.masks import make_identity

F32 = mybir.dt.float32
BF16 = mybir.dt.bfloat16
U32 = mybir.dt.uint32
U8 = mybir.dt.uint8
E4M3X4 = mybir.dt.float8_e4m3fn_x4
E5M2X4 = mybir.dt.float8_e5m2_x4

BATCH, SEQ, D_IN, D_OUT = 3, 512, 256, 8192
TOKENS = BATCH * SEQ

P = 128
PACK = 4
K_PASS = P * PACK
PASSES = D_OUT // K_PASS
GROUP = 512
GROUPS = TOKENS // GROUP
HALF = GROUP // 2
M_TILES = D_IN // P
PLANE = K_PASS // 4

CHUNK_PASSES = 4
CHUNK_K = CHUNK_PASSES * K_PASS
K_CHUNKS = PASSES // CHUNK_PASSES
TOGETHER = 2
PSUM_BANKS = 8
CHUNKS_AHEAD = 5
PAD = 8

FLOPS = 2 * TOKENS * D_OUT * D_IN
BYTES = 2 * TOKENS * D_OUT + 2 * D_OUT * D_IN + 4 * TOKENS * D_IN


def tile_relativemultiheadattention_pa_k_kernel(tc, pos_embed, W_r, b_r, grad_out, out):
    nc = tc.nc
    grad_rows = grad_out.flatten_outer_dims()
    out_rows = out.flatten_outer_dims()
    assert SEQ == GROUP

    chunks = [(n, q) for q in range(K_CHUNKS) for n in range(TOGETHER)]
    chunks += [(n, q) for n in range(TOGETHER, GROUPS) for q in range(K_CHUNKS)]

    with ExitStack() as ctx:
        keep = ctx.enter_context(tc.tile_pool(name="keep", bufs=1))
        grad_pool = ctx.enter_context(tc.tile_pool(name="grad", bufs=2 * CHUNKS_AHEAD))
        w_raw_pool = ctx.enter_context(tc.tile_pool(name="w_raw", bufs=K_CHUNKS))
        w_grouped_pool = ctx.enter_context(tc.tile_pool(name="w_grouped", bufs=2))
        grouped_pool = ctx.enter_context(tc.tile_pool(name="grouped", bufs=CHUNK_PASSES + 2))
        operand_pool = ctx.enter_context(tc.tile_pool(name="operand", bufs=2 * CHUNK_PASSES + 1))
        result_pool = ctx.enter_context(tc.tile_pool(name="result", bufs=4))
        acc_pool = ctx.enter_context(tc.psum_pool(name="acc", bufs=TOGETHER))
        bank_pool = ctx.enter_context(tc.psum_pool(name="bank", bufs=PSUM_BANKS - TOGETHER * M_TILES))
        ctx.enter_context(tc.manual_schedule())

        identity = keep.tile([P, P], F32, name="identity")
        make_identity(nc, identity[:])

        w_codes = keep.tile([P, PASSES, D_IN], U32, name="w_codes", align_bytes=64)
        w_scales = keep.tile([P, PASSES, D_IN], U8, name="w_scales", align_bytes=64)

        g_t = [keep.tile([P, PAD + TOKENS], F32, name="g_t%d" % m) for m in range(M_TILES)]
        for m in range(M_TILES):
            nc.vector.memset(g_t[m][:, 0:PAD], 0.0)

        w_raw = {}
        grad_raw = {}
        acc = {}

        def load_chunk(i):
            n, q = chunks[i]
            k_range = slice(q * CHUNK_K, (q + 1) * CHUNK_K)
            if n == 0:
                raw = w_raw_pool.tile([P, CHUNK_PASSES, PACK, D_IN], BF16, name="w_raw")
                nc.sync.dma_start(
                    out=raw[:].rearrange("p g (u e) d -> p (g u) (e d)", e=2),
                    in_=W_r[k_range, :].rearrange("(g u p e) d -> p (g u) (e d)", u=2, p=P, e=2),
                )
                w_raw[q] = raw
            grad_raw[i] = []
            for h in range(GROUP // HALF):
                raw = grad_pool.tile([P, HALF // P, CHUNK_K], BF16, name="grad_raw")
                row0 = n * GROUP + h * HALF
                nc.sync.dma_start(
                    out=raw[:],
                    in_=grad_rows[row0 : row0 + HALF, k_range].rearrange("(s p) k -> p s k", p=P),
                )
                grad_raw[i].append(raw)

        def regroup_weights(q):
            grouped = w_grouped_pool.tile([P, CHUNK_PASSES, D_IN, PACK], BF16, name="w_grouped", align_bytes=64)
            for j in range(CHUNK_PASSES):
                nc.vector.tensor_copy(
                    out=grouped[:, j, :, :].rearrange("p (c i) t -> p c t i", i=4),
                    in_=w_raw[q][:, j, :, :].rearrange("p t (c i) -> p c t i", i=4),
                )
            return grouped

        def quantise_weights(q, grouped):
            passes = slice(q * CHUNK_PASSES, (q + 1) * CHUNK_PASSES)
            nc.vector.quantize_mx(
                out=w_codes[:, passes, :].rearrange("p c d -> p (c d)").bitcast(E4M3X4),
                scales=w_scales[:, passes, :].rearrange("p c d -> p (c d)"),
                in_=grouped[:].rearrange("p c d t -> p (c d t)"),
            )

        def transpose_chunk(i):
            n, q = chunks[i]
            grouped = [
                grouped_pool.tile([P, GROUP, PACK], BF16, name="grouped", align_bytes=64)
                for j in range(CHUNK_PASSES)
            ]
            operands = []

            def quantise_pass(j):
                codes = operand_pool.tile([P, GROUP], U32, name="grad_codes", align_bytes=64)
                scales = operand_pool.tile([P, GROUP], U8, name="grad_scales", align_bytes=64)
                nc.vector.quantize_mx(
                    out=codes[:].bitcast(E5M2X4),
                    scales=scales[:],
                    in_=grouped[j][:].rearrange("p r t -> p (r t)"),
                )
                operands.append((q * CHUNK_PASSES + j, codes, scales))

            for h in range(GROUP // HALF):
                for j in range(CHUNK_PASSES):
                    bank = bank_pool.tile([P, 2, HALF], F32, name="bank")
                    for u in range(2):
                        for s in range(HALF // P):
                            word0 = (2 * j + u) * PLANE
                            nc.tensor.transpose(
                                bank[:, u, s * P : (s + 1) * P],
                                grad_raw[i][h][:, s, :].bitcast(F32)[:, word0 : word0 + PLANE],
                                identity[:],
                            )
                    pairs = (
                        grouped[j][:, h * HALF : (h + 1) * HALF, :]
                        .rearrange("p r t -> p (r t)")
                        .bitcast(F32)
                        .rearrange("p (r u) -> p r u", u=2)
                    )
                    if n >= TOGETHER and j == CHUNK_PASSES - 1:
                        nc.vector.tensor_copy(out=pairs, in_=bank[:].rearrange("p u r -> p r u"))
                    else:
                        nc.scalar.copy(out=pairs, in_=bank[:].rearrange("p u r -> p r u"))
                    if h == 1 and j > 0:
                        quantise_pass(j - 1)
            quantise_pass(CHUNK_PASSES - 1)
            return operands

        def multiply_chunk(i, operands):
            n, q = chunks[i]
            if q == 0:
                acc[n] = [acc_pool.tile([P, GROUP], F32, name="acc%d" % m) for m in range(M_TILES)]
            for m in range(M_TILES):
                columns = slice(m * P, (m + 1) * P)
                for c, codes, scales in operands:
                    nc.tensor.matmul_mx(
                        out=acc[n][m][:],
                        lhsT=w_codes[:, c, columns].bitcast(E4M3X4),
                        lhsT_scale=w_scales[:, c, columns],
                        rhs=codes[:].bitcast(E5M2X4),
                        rhs_scale=scales[:],
                        start=(c == 0),
                        stop=(c == PASSES - 1),
                    )
                if q == K_CHUNKS - 1:
                    done = g_t[m][:, PAD + n * GROUP : PAD + (n + 1) * GROUP]
                    if m == 0:
                        nc.scalar.copy(out=done, in_=acc[n][m][:])
                    else:
                        nc.vector.tensor_copy(out=done, in_=acc[n][m][:])

        def store_batch(b):
            banks = [bank_pool.tile([P, 2, D_IN], F32, name="bank") for pair in range(2)]
            for m in range(M_TILES):
                for pair in range(2):
                    for j in range(2):
                        s0 = (2 * pair + j) * P
                        col0 = PAD + (SEQ + 1) * b + s0 - 2
                        nc.tensor.transpose(
                            banks[pair][:, j, m * P : (m + 1) * P],
                            g_t[m][:, col0 : col0 + P],
                            identity[:],
                        )
            for pair in range(2):
                result = result_pool.tile([P, 2, D_IN], F32, name="result")
                if pair == 0:
                    nc.scalar.copy(out=result[:], in_=banks[pair][:])
                else:
                    nc.vector.tensor_copy(out=result[:], in_=banks[pair][:])
                row0 = b * SEQ + pair * 2 * P
                nc.sync.dma_start(
                    out=out_rows[row0 : row0 + 2 * P, :].rearrange("(j p) d -> p j d", p=P),
                    in_=result[:],
                )

        for i in range(CHUNKS_AHEAD):
            load_chunk(i)

        waiting = None
        complete = []
        for i in range(len(chunks)):
            n, q = chunks[i]
            if n == 0:
                w_grouped = regroup_weights(q)
            operands = transpose_chunk(i)
            if n == 0:
                quantise_weights(q, w_grouped)
            if i + CHUNKS_AHEAD < len(chunks):
                load_chunk(i + CHUNKS_AHEAD)
            for b in complete:
                store_batch(b)
            complete = []
            if i > 0:
                multiply_chunk(i - 1, waiting)
                if chunks[i - 1][1] == K_CHUNKS - 1:
                    complete.append(chunks[i - 1][0])
            waiting = operands
        multiply_chunk(len(chunks) - 1, waiting)
        store_batch(GROUPS - 1)
